import numpy as np
import ml_dtypes


def mxq(x, axis, fmt="e4m3"):
    dtype, down = {"e4m3": (ml_dtypes.float8_e4m3fn, 7), "e5m2": (ml_dtypes.float8_e5m2, 14)}[fmt]
    v = np.moveaxis(np.asarray(x, np.float32).astype(ml_dtypes.bfloat16).astype(np.float64), axis, -1)
    blocks = v.reshape(v.shape[:-1] + (-1, 32))
    amax = np.abs(blocks).max(-1, keepdims=True)
    byte = np.maximum(np.where(amax > 0, np.frexp(amax)[1] - 1 + 127, 0) - down, 1)
    scale = np.exp2(byte - 127.0)
    codes = (blocks / scale).astype(np.float32).astype(dtype).astype(np.float64)
    return np.moveaxis((codes * scale).reshape(v.shape), -1, axis)


WIDE = False


def mx_kscale(k):
    if not WIDE:
        return np.ones(k)
    levels = np.array([10, -10, 5, -5, 0])
    a = np.random.permutation(np.resize(levels, k // 512 * 4)).reshape(k // 512, 4)
    idx = np.arange(k)
    return np.exp2(a[idx // 512, idx % 128 // 32])


BF16 = ml_dtypes.bfloat16


def bf(x):
    return np.asarray(x, np.float32).astype(BF16)


def f64(x):
    return np.asarray(x).astype(np.float64)


M, P, D = 512, 512, 512
GAMMAK = 1.0 / 256.0
SIG = np.sqrt(1.0 / (GAMMAK * D))


def setup_inputs():
    s = mx_kscale(D)
    return {"x_base": bf(np.random.standard_normal((M, D)) * SIG),
            "y": bf(np.random.standard_normal((P, D)) * SIG * s),
            "R": bf((np.eye(D) + np.random.standard_normal((D, D)) * 0.5 / np.sqrt(D)) / s[None, :]),
            "t": bf(np.random.standard_normal((D, 1)) * 0.4 * SIG)}


def reference(x_base, y, R, t):
    xb = f64(x_base)
    yt = (mxq(f64(y), 1, "e4m3") @ mxq(f64(R), 1, "e4m3").T) + f64(t)[:, 0]
    cross = mxq(xb, 1, "e4m3") @ mxq(yt, 1, "e4m3").T
    sq = np.maximum(np.sum(xb * xb, axis=1)[:, None] + np.sum(yt * yt, axis=1)[None, :] - 2.0 * cross, 0.0)
    return np.exp(-GAMMAK * sq)

@@ -1,0 +1,196 @@
+from contextlib import ExitStack
+
+import concourse.mybir as mybir
+from concourse.masks import make_identity
+
+F32 = mybir.dt.float32
+BF16 = mybir.dt.bfloat16
+U32 = mybir.dt.uint32
+U8 = mybir.dt.uint8
+FP8X4 = mybir.dt.float8_e4m3fn_x4
+ALU = mybir.AluOpType
+ACT = mybir.ActivationFunctionType
+
+P = 128
+PACK = 4
+SIZE = 512
+TILES = SIZE // P
+PAIR = 2 * P
+GAMMA = 1.0 / 256.0
+
+FLOPS = 2 * 2 * SIZE * SIZE * SIZE
+
+
+def tile_nntransformlearner_pa_s_kernel(tc, x_base, y, R, t, out):
+    nc = tc.nc
+    with ExitStack() as ctx:
+        keep = ctx.enter_context(tc.tile_pool(name="keep", bufs=1))
+        stage = ctx.enter_context(tc.tile_pool(name="stage", bufs=4))
+        psum = ctx.enter_context(tc.psum_pool(name="psum", bufs=8))
+        ctx.enter_context(tc.manual_schedule())
+
+        y_sb = keep.tile([P, TILES, SIZE], BF16, name="y_sb")
+        r_sb = keep.tile([P, TILES, SIZE], BF16, name="r_sb")
+        x_sb = keep.tile([P, TILES, SIZE], BF16, name="x_sb")
+        t_sb = keep.tile([P, PACK], BF16, name="t_sb")
+        nc.scalar.dma_start(
+            out=t_sb[:].rearrange("p (u e) -> p u e", u=2),
+            in_=t.rearrange("(u p e) o -> p u (e o)", u=2, e=2),
+        )
+        y_rows = y.rearrange("(h a p) k -> h p a k", h=2, p=P)
+        r_rows = R.rearrange("(u p e) k -> u p (e k)", u=2, e=2)
+        x_rows = x_base.rearrange("(p h a) d -> h p (a d)", h=2, a=2)
+        out_rows = out.rearrange("(p a) j -> a p j", a=TILES)
+        for h in range(2):
+            nc.sync.dma_start(out=y_sb[:, 2 * h : 2 * h + 2, :], in_=y_rows[h])
+        for h in range(2):
+            nc.sync.dma_start(out=r_sb[:, 2 * h : 2 * h + 2, :].rearrange("p e k -> p (e k)"), in_=r_rows[h])
+        for h in range(2):
+            nc.sync.dma_start(out=x_sb[:, 2 * h : 2 * h + 2, :].rearrange("p a d -> p (a d)"), in_=x_rows[h])
+
+        ident = keep.tile([P, P], F32, name="ident")
+        make_identity(nc, ident[:])
+        ones = keep.tile([P, P], F32, name="ones")
+        nc.vector.memset(ones[:], 1.0)
+        warm = keep.tile([P, 1], F32, name="warm")
+        nc.vector.memset(warm[:], 0.0)
+        nc.scalar.activation(out=warm[:], in_=warm[:], func=ACT.Exp)
+        t32 = keep.tile([P, PACK], F32, name="t32")
+        nc.vector.tensor_copy(out=t32[:], in_=t_sb[:])
+
+        def flip(rows_sb, h):
+            flipped = psum.tile([P, 2, PAIR], F32, name="flipped", tag="bank")
+            for a in range(2):
+                row_words = rows_sb[:, 2 * h + a, :].bitcast(F32)
+                for u in range(2):
+                    nc.tensor.transpose(
+                        flipped[:, u, a * P : (a + 1) * P], row_words[:, u * P : (u + 1) * P], ident[:]
+                    )
+            return flipped
+
+        def operand(name):
+            grouped = keep.tile([P, SIZE * PACK], BF16, align_bytes=64, name=name + "_grouped")
+            codes = keep.tile([P, SIZE], U32, align_bytes=64, name=name + "_codes")
+            scales = keep.tile([P, SIZE], U8, align_bytes=64, name=name + "_scales")
+            return grouped, codes, scales
+
+        def regroup(copy, flipped, mx, h):
+            words = mx[0][:].bitcast(F32).rearrange("p (c u) -> p c u", u=2)
+            copy(out=words[:, h * PAIR : (h + 1) * PAIR, :], in_=flipped[:].rearrange("p u c -> p c u"))
+
+        def quantise(mx, h):
+            grouped, codes, scales = mx
+            cols = slice(h * PAIR, (h + 1) * PAIR)
+            nc.vector.quantize_mx(
+                out=codes[:, cols].bitcast(FP8X4),
+                scales=scales[:, cols],
+                in_=grouped[:, h * PAIR * PACK : (h + 1) * PAIR * PACK],
+            )
+
+        y_mx = operand("y")
+        r_mx = operand("r")
+        x_mx = operand("x")
+        yt_mx = operand("yt")
+        y_flipped = [flip(y_sb, h) for h in range(2)]
+        r_flipped = [flip(r_sb, h) for h in range(2)]
+        x_flipped = [flip(x_sb, h) for h in range(2)]
+        regroup(nc.vector.tensor_copy, y_flipped[0], y_mx, 0)
+        regroup(nc.scalar.copy, y_flipped[1], y_mx, 1)
+        quantise(y_mx, 0)
+        quantise(y_mx, 1)
+        regroup(nc.vector.tensor_copy, r_flipped[0], r_mx, 0)
+        regroup(nc.scalar.copy, r_flipped[1], r_mx, 1)
+        quantise(r_mx, 0)
+        regroup(nc.vector.tensor_copy, x_flipped[0], x_mx, 0)
+        quantise(r_mx, 1)
+        regroup(nc.vector.tensor_copy, x_flipped[1], x_mx, 1)
+        quantise(x_mx, 0)
+        quantise(x_mx, 1)
+
+        def mx_pass(acc, lhs, lhs_cols, rhs, rhs_cols):
+            nc.tensor.matmul_mx(
+                out=acc,
+                lhsT=lhs[1][:, lhs_cols].bitcast(FP8X4),
+                lhsT_scale=lhs[2][:, lhs_cols],
+                rhs=rhs[1][:, rhs_cols].bitcast(FP8X4),
+                rhs_scale=rhs[2][:, rhs_cols],
+                start=True,
+                stop=True,
+            )
+
+        def tile_cols(i):
+            return slice(i * P, (i + 1) * P)
+
+        every = slice(0, SIZE)
+
+        by_feature = []
+        for m in range(PACK):
+            acc = psum.tile([P, SIZE], F32, name="by_feature", tag="bank")
+            mx_pass(acc[:], r_mx, tile_cols(m), y_mx, every)
+            by_feature.append(acc)
+        by_point = []
+        for b in range(TILES):
+            acc = psum.tile([P, PACK, P], F32, name="by_point", tag="bank")
+            for m in range(PACK):
+                mx_pass(acc[:, m, :], r_mx, tile_cols(m), y_mx, tile_cols(b))
+            by_point.append(acc)
+
+        squares = []
+        for m in range(PACK):
+            sq = keep.tile([P, SIZE], F32, name="sq%d" % m)
+            nc.scalar.activation(out=sq[:], in_=by_feature[m][:], func=ACT.Square, bias=t32[:, m : m + 1])
+            squares.append(sq)
+        yn_acc = [psum.tile([P, PAIR], F32, name="yn_acc", tag="bank") for h in range(2)]
+        for pair in range(2):
+            for h in range(2):
+                cols = slice(h * PAIR, (h + 1) * PAIR)
+                nc.gpsimd.tensor_tensor(
+                    out=squares[2 * pair][:, cols],
+                    in0=squares[2 * pair][:, cols],
+                    in1=squares[2 * pair + 1][:, cols],
+                    op=ALU.add,
+                )
+                nc.tensor.matmul(
+                    out=yn_acc[h][:], lhsT=ones[:], rhs=squares[2 * pair][:, cols], start=(pair == 0), stop=(pair == 1)
+                )
+
+        yt_grouped = yt_mx[0][:].rearrange("p (j m) -> p j m", m=PACK)
+        for b in range(TILES):
+            nc.vector.tensor_tensor(
+                out=yt_grouped[:, tile_cols(b), :],
+                in0=by_point[b][:].rearrange("p m j -> p j m"),
+                in1=t32[:].unsqueeze(1).to_broadcast([P, P, PACK]),
+                op=ALU.add,
+            )
+        quantise(yt_mx, 0)
+        quantise(yt_mx, 1)
+
+        xn = keep.tile([P, TILES], F32, name="xn")
+        for a in range(TILES):
+            unused = stage.tile([P, SIZE], BF16, name="unused")
+            nc.scalar.activation(out=unused[:], in_=x_sb[:, a, :], func=ACT.Square, accum_out=xn[:, a : a + 1])
+        yn = keep.tile([P, SIZE], F32, name="yn")
+        for h in range(2):
+            nc.vector.tensor_copy(out=yn[:, h * PAIR : (h + 1) * PAIR], in_=yn_acc[h][:])
+        xn_scaled = keep.tile([P, TILES], F32, name="xn_scaled")
+        nc.vector.tensor_scalar_mul(out=xn_scaled[:], in0=xn[:], scalar1=-GAMMA)
+
+        crosses = []
+        for a in range(TILES):
+            cross = psum.tile([P, SIZE], F32, name="cross", tag="bank")
+            mx_pass(cross[:], x_mx, tile_cols(a), yt_mx, every)
+            crosses.append(cross)
+        results = []
+        for a in range(TILES + 1):
+            if a < TILES:
+                part = stage.tile([P, SIZE], F32, name="part")
+                nc.vector.scalar_tensor_tensor(
+                    out=part[:], in0=crosses[a][:], scalar=-2.0, in1=yn[:], op0=ALU.mult, op1=ALU.add
+                )
+                g = stage.tile([P, SIZE], F32, name="g")
+                nc.scalar.activation(out=g[:], in_=part[:], func=ACT.Exp, scale=-GAMMA, bias=xn_scaled[:, a : a + 1])
+                results.append(g)
+            if a > 0:
+                g = results[a - 1]
+                nc.vector.tensor_scalar_min(out=g[:], in0=g[:], scalar1=1.0)
+                nc.sync.dma_start(out=out_rows[a - 1], in_=g[:])

@@ -50,8 +50,11 @@ def tile_nntransformlearner_pa_s_kernel(tc, x_base, y, R, t, out):
 
         ident = keep.tile([P, P], F32, name="ident")
         make_identity(nc, ident[:])
-        ones = keep.tile([P, P], F32, name="ones")
+        ones = keep.tile([P, PAIR], F32, name="ones")
         nc.vector.memset(ones[:], 1.0)
+        idle = psum.tile([P, PAIR], F32, name="idle", tag="bank")
+        for rep in range(2):
+            nc.tensor.matmul(out=idle[:], lhsT=ones[:, 0:P], rhs=ones[:], start=True, stop=True)
         warm = keep.tile([P, 1], F32, name="warm")
         nc.vector.memset(warm[:], 0.0)
         nc.scalar.activation(out=warm[:], in_=warm[:], func=ACT.Exp)
@@ -151,7 +154,7 @@ def tile_nntransformlearner_pa_s_kernel(tc, x_base, y, R, t, out):
                     op=ALU.add,
                 )
                 nc.tensor.matmul(
-                    out=yn_acc[h][:], lhsT=ones[:], rhs=squares[2 * pair][:, cols], start=(pair == 0), stop=(pair == 1)
+                    out=yn_acc[h][:], lhsT=ones[:, 0:P], rhs=squares[2 * pair][:, cols], start=(pair == 0), stop=(pair == 1)
                 )
 
         yt_grouped = yt_mx[0][:].rearrange("p (j m) -> p j m", m=PACK)

@@ -17,6 +17,7 @@ SIZE = 512
 TILES = SIZE // P
 PAIR = 2 * P
 GAMMA = 1.0 / 256.0
+LAG = 2
 
 FLOPS = 2 * 2 * SIZE * SIZE * SIZE
 
@@ -101,14 +102,12 @@ def tile_nntransformlearner_pa_s_kernel(tc, x_base, y, R, t, out):
         regroup(nc.scalar.copy, y_flipped[1], y_mx, 1)
         quantise(y_mx, 0)
         quantise(y_mx, 1)
-        regroup(nc.vector.tensor_copy, r_flipped[0], r_mx, 0)
+        regroup(nc.scalar.copy, r_flipped[0], r_mx, 0)
         regroup(nc.scalar.copy, r_flipped[1], r_mx, 1)
         quantise(r_mx, 0)
-        regroup(nc.vector.tensor_copy, x_flipped[0], x_mx, 0)
         quantise(r_mx, 1)
+        regroup(nc.scalar.copy, x_flipped[0], x_mx, 0)
         regroup(nc.vector.tensor_copy, x_flipped[1], x_mx, 1)
-        quantise(x_mx, 0)
-        quantise(x_mx, 1)
 
         def mx_pass(acc, lhs, lhs_cols, rhs, rhs_cols):
             nc.tensor.matmul_mx(
@@ -127,22 +126,61 @@ def tile_nntransformlearner_pa_s_kernel(tc, x_base, y, R, t, out):
         every = slice(0, SIZE)
 
         by_feature = []
-        for m in range(PACK):
+        by_point = []
+
+        def feature_pass(m):
             acc = psum.tile([P, SIZE], F32, name="by_feature", tag="bank")
             mx_pass(acc[:], r_mx, tile_cols(m), y_mx, every)
             by_feature.append(acc)
-        by_point = []
-        for b in range(TILES):
+
+        def point_passes(b):
             acc = psum.tile([P, PACK, P], F32, name="by_point", tag="bank")
             for m in range(PACK):
                 mx_pass(acc[:, m, :], r_mx, tile_cols(m), y_mx, tile_cols(b))
             by_point.append(acc)
 
+        feature_pass(0)
+        feature_pass(1)
+        point_passes(0)
+        feature_pass(2)
+        point_passes(1)
+        feature_pass(3)
+        point_passes(2)
+        point_passes(3)
+
         squares = []
         for m in range(PACK):
             sq = keep.tile([P, SIZE], F32, name="sq%d" % m)
-            nc.scalar.activation(out=sq[:], in_=by_feature[m][:], func=ACT.Square, bias=t32[:, m : m + 1])
             squares.append(sq)
+
+        def square(m, cols):
+            nc.scalar.activation(
+                out=squares[m][:, cols], in_=by_feature[m][:, cols], func=ACT.Square, bias=t32[:, m : m + 1]
+            )
+
+        for pair in range(2):
+            for h in range(2):
+                for m in (2 * pair, 2 * pair + 1):
+                    square(m, slice(h * PAIR, (h + 1) * PAIR))
+        xn = keep.tile([P, TILES], F32, name="xn")
+        for a in range(TILES):
+            unused = stage.tile([P, SIZE], BF16, name="unused")
+            nc.scalar.activation(out=unused[:], in_=x_sb[:, a, :], func=ACT.Square, accum_out=xn[:, a : a + 1])
+
+        yt_grouped = yt_mx[0][:].rearrange("p (j m) -> p j m", m=PACK)
+        for b in range(TILES):
+            nc.vector.tensor_tensor(
+                out=yt_grouped[:, tile_cols(b), :],
+                in0=by_point[b][:].rearrange("p m j -> p j m"),
+                in1=t32[:].unsqueeze(1).to_broadcast([P, P, PACK]),
+                op=ALU.add,
+            )
+            if b == 2:
+                quantise(yt_mx, 0)
+        quantise(x_mx, 0)
+        quantise(yt_mx, 1)
+        quantise(x_mx, 1)
+
         yn_acc = [psum.tile([P, PAIR], F32, name="yn_acc", tag="bank") for h in range(2)]
         for pair in range(2):
             for h in range(2):
@@ -156,27 +194,11 @@ def tile_nntransformlearner_pa_s_kernel(tc, x_base, y, R, t, out):
                 nc.tensor.matmul(
                     out=yn_acc[h][:], lhsT=ones[:, 0:P], rhs=squares[2 * pair][:, cols], start=(pair == 0), stop=(pair == 1)
                 )
-
-        yt_grouped = yt_mx[0][:].rearrange("p (j m) -> p j m", m=PACK)
-        for b in range(TILES):
-            nc.vector.tensor_tensor(
-                out=yt_grouped[:, tile_cols(b), :],
-                in0=by_point[b][:].rearrange("p m j -> p j m"),
-                in1=t32[:].unsqueeze(1).to_broadcast([P, P, PACK]),
-                op=ALU.add,
-            )
-        quantise(yt_mx, 0)
-        quantise(yt_mx, 1)
-
-        xn = keep.tile([P, TILES], F32, name="xn")
-        for a in range(TILES):
-            unused = stage.tile([P, SIZE], BF16, name="unused")
-            nc.scalar.activation(out=unused[:], in_=x_sb[:, a, :], func=ACT.Square, accum_out=xn[:, a : a + 1])
+        xn_scaled = keep.tile([P, TILES], F32, name="xn_scaled")
+        nc.gpsimd.tensor_scalar_mul(out=xn_scaled[:], in0=xn[:], scalar1=-GAMMA)
         yn = keep.tile([P, SIZE], F32, name="yn")
         for h in range(2):
             nc.vector.tensor_copy(out=yn[:, h * PAIR : (h + 1) * PAIR], in_=yn_acc[h][:])
-        xn_scaled = keep.tile([P, TILES], F32, name="xn_scaled")
-        nc.vector.tensor_scalar_mul(out=xn_scaled[:], in0=xn[:], scalar1=-GAMMA)
 
         crosses = []
         for a in range(TILES):
@@ -184,7 +206,7 @@ def tile_nntransformlearner_pa_s_kernel(tc, x_base, y, R, t, out):
             mx_pass(cross[:], x_mx, tile_cols(a), yt_mx, every)
             crosses.append(cross)
         results = []
-        for a in range(TILES + 1):
+        for a in range(TILES + LAG):
             if a < TILES:
                 part = stage.tile([P, SIZE], F32, name="part")
                 nc.vector.scalar_tensor_tensor(
@@ -193,7 +215,7 @@ def tile_nntransformlearner_pa_s_kernel(tc, x_base, y, R, t, out):
                 g = stage.tile([P, SIZE], F32, name="g")
                 nc.scalar.activation(out=g[:], in_=part[:], func=ACT.Exp, scale=-GAMMA, bias=xn_scaled[:, a : a + 1])
                 results.append(g)
-            if a > 0:
-                g = results[a - 1]
+            if a >= LAG:
+                g = results[a - LAG]
                 nc.vector.tensor_scalar_min(out=g[:], in0=g[:], scalar1=1.0)
-                nc.sync.dma_start(out=out_rows[a - 1], in_=g[:])
+                nc.sync.dma_start(out=out_rows[a - LAG], in_=g[:])

@@ -205,17 +205,21 @@ def tile_nntransformlearner_pa_s_kernel(tc, x_base, y, R, t, out):
             cross = psum.tile([P, SIZE], F32, name="cross", tag="bank")
             mx_pass(cross[:], x_mx, tile_cols(a), yt_mx, every)
             crosses.append(cross)
+        pieces = [(a, every) for a in range(TILES - 1)]
+        pieces.extend([(TILES - 1, slice(h * PAIR, (h + 1) * PAIR)) for h in range(2)])
         results = []
-        for a in range(TILES + LAG):
-            if a < TILES:
-                part = stage.tile([P, SIZE], F32, name="part")
+        for k in range(len(pieces) + LAG):
+            if k < len(pieces):
+                a, cols = pieces[k]
+                part = stage.tile([P, cols.stop - cols.start], F32, name="part")
                 nc.vector.scalar_tensor_tensor(
-                    out=part[:], in0=crosses[a][:], scalar=-2.0, in1=yn[:], op0=ALU.mult, op1=ALU.add
+                    out=part[:], in0=crosses[a][:, cols], scalar=-2.0, in1=yn[:, cols], op0=ALU.mult, op1=ALU.add
                 )
-                g = stage.tile([P, SIZE], F32, name="g")
+                g = stage.tile([P, cols.stop - cols.start], F32, name="g")
                 nc.scalar.activation(out=g[:], in_=part[:], func=ACT.Exp, scale=-GAMMA, bias=xn_scaled[:, a : a + 1])
                 results.append(g)
-            if a >= LAG:
-                g = results[a - LAG]
+            if k >= LAG:
+                a, cols = pieces[k - LAG]
+                g = results[k - LAG]
                 nc.vector.tensor_scalar_min(out=g[:], in0=g[:], scalar1=1.0)
-                nc.sync.dma_start(out=out_rows[a - LAG], in_=g[:])
+                nc.sync.dma_start(out=out_rows[a][:, cols], in_=g[:])

@@ -108,6 +108,8 @@ def tile_nntransformlearner_pa_s_kernel(tc, x_base, y, R, t, out):
         quantise(r_mx, 1)
         regroup(nc.scalar.copy, x_flipped[0], x_mx, 0)
         regroup(nc.vector.tensor_copy, x_flipped[1], x_mx, 1)
+        quantise(x_mx, 0)
+        quantise(x_mx, 1)
 
         def mx_pass(acc, lhs, lhs_cols, rhs, rhs_cols):
             nc.tensor.matmul_mx(
@@ -139,14 +141,10 @@ def tile_nntransformlearner_pa_s_kernel(tc, x_base, y, R, t, out):
                 mx_pass(acc[:, m, :], r_mx, tile_cols(m), y_mx, tile_cols(b))
             by_point.append(acc)
 
-        feature_pass(0)
-        feature_pass(1)
-        point_passes(0)
-        feature_pass(2)
-        point_passes(1)
-        feature_pass(3)
-        point_passes(2)
-        point_passes(3)
+        for m in range(PACK):
+            feature_pass(m)
+        for b in range(TILES):
+            point_passes(b)
 
         squares = []
         for m in range(PACK):
@@ -175,11 +173,8 @@ def tile_nntransformlearner_pa_s_kernel(tc, x_base, y, R, t, out):
                 in1=t32[:].unsqueeze(1).to_broadcast([P, P, PACK]),
                 op=ALU.add,
             )
-            if b == 2:
-                quantise(yt_mx, 0)
-        quantise(x_mx, 0)
+        quantise(yt_mx, 0)
         quantise(yt_mx, 1)
-        quantise(x_mx, 1)
 
         yn_acc = [psum.tile([P, PAIR], F32, name="yn_acc", tag="bank") for h in range(2)]
         for pair in range(2):
@@ -211,11 +206,11 @@ def tile_nntransformlearner_pa_s_kernel(tc, x_base, y, R, t, out):
         for k in range(len(pieces) + LAG):
             if k < len(pieces):
                 a, cols = pieces[k]
-                part = stage.tile([P, cols.stop - cols.start], F32, name="part")
+                part = keep.tile([P, cols.stop - cols.start], F32, name="part%d" % k)
                 nc.vector.scalar_tensor_tensor(
                     out=part[:], in0=crosses[a][:, cols], scalar=-2.0, in1=yn[:, cols], op0=ALU.mult, op1=ALU.add
                 )
-                g = stage.tile([P, cols.stop - cols.start], F32, name="g")
+                g = keep.tile([P, cols.stop - cols.start], F32, name="g%d" % k)
                 nc.scalar.activation(out=g[:], in_=part[:], func=ACT.Exp, scale=-GAMMA, bias=xn_scaled[:, a : a + 1])
                 results.append(g)
             if k >= LAG:

@@ -109,7 +109,6 @@ def tile_nntransformlearner_pa_s_kernel(tc, x_base, y, R, t, out):
         regroup(nc.scalar.copy, x_flipped[0], x_mx, 0)
         regroup(nc.vector.tensor_copy, x_flipped[1], x_mx, 1)
         quantise(x_mx, 0)
-        quantise(x_mx, 1)
 
         def mx_pass(acc, lhs, lhs_cols, rhs, rhs_cols):
             nc.tensor.matmul_mx(
@@ -141,10 +140,14 @@ def tile_nntransformlearner_pa_s_kernel(tc, x_base, y, R, t, out):
                 mx_pass(acc[:, m, :], r_mx, tile_cols(m), y_mx, tile_cols(b))
             by_point.append(acc)
 
-        for m in range(PACK):
-            feature_pass(m)
-        for b in range(TILES):
-            point_passes(b)
+        feature_pass(0)
+        feature_pass(1)
+        point_passes(0)
+        feature_pass(2)
+        point_passes(1)
+        feature_pass(3)
+        point_passes(2)
+        point_passes(3)
 
         squares = []
         for m in range(PACK):
@@ -173,14 +176,13 @@ def tile_nntransformlearner_pa_s_kernel(tc, x_base, y, R, t, out):
                 in1=t32[:].unsqueeze(1).to_broadcast([P, P, PACK]),
                 op=ALU.add,
             )
-        quantise(yt_mx, 0)
-        quantise(yt_mx, 1)
 
         yn_acc = [psum.tile([P, PAIR], F32, name="yn_acc", tag="bank") for h in range(2)]
         for pair in range(2):
             for h in range(2):
                 cols = slice(h * PAIR, (h + 1) * PAIR)
-                nc.gpsimd.tensor_tensor(
+                adder = nc.vector if (pair, h) == (1, 1) else nc.gpsimd
+                adder.tensor_tensor(
                     out=squares[2 * pair][:, cols],
                     in0=squares[2 * pair][:, cols],
                     in1=squares[2 * pair + 1][:, cols],
@@ -189,8 +191,14 @@ def tile_nntransformlearner_pa_s_kernel(tc, x_base, y, R, t, out):
                 nc.tensor.matmul(
                     out=yn_acc[h][:], lhsT=ones[:, 0:P], rhs=squares[2 * pair][:, cols], start=(pair == 0), stop=(pair == 1)
                 )
+        quantise(yt_mx, 0)
+        quantise(yt_mx, 1)
+        quantise(x_mx, 1)
         xn_scaled = keep.tile([P, TILES], F32, name="xn_scaled")
-        nc.gpsimd.tensor_scalar_mul(out=xn_scaled[:], in0=xn[:], scalar1=-GAMMA)
+        for h in range(2):
+            nc.gpsimd.tensor_scalar_mul(
+                out=xn_scaled[:, 2 * h : 2 * h + 2], in0=xn[:, 2 * h : 2 * h + 2], scalar1=-GAMMA
+            )
         yn = keep.tile([P, SIZE], F32, name="yn")
         for h in range(2):
             nc.vector.tensor_copy(out=yn[:, h * PAIR : (h + 1) * PAIR], in_=yn_acc[h][:])

@@ -168,6 +168,22 @@ def tile_nntransformlearner_pa_s_kernel(tc, x_base, y, R, t, out):
             unused = stage.tile([P, SIZE], BF16, name="unused")
             nc.scalar.activation(out=unused[:], in_=x_sb[:, a, :], func=ACT.Square, accum_out=xn[:, a : a + 1])
 
+        yn_acc = [psum.tile([P, PAIR], F32, name="yn_acc", tag="bank") for h in range(2)]
+
+        def add_squares(adder, pair, h):
+            cols = slice(h * PAIR, (h + 1) * PAIR)
+            adder.tensor_tensor(
+                out=squares[2 * pair][:, cols],
+                in0=squares[2 * pair][:, cols],
+                in1=squares[2 * pair + 1][:, cols],
+                op=ALU.add,
+            )
+            nc.tensor.matmul(
+                out=yn_acc[h][:], lhsT=ones[:, 0:P], rhs=squares[2 * pair][:, cols], start=(pair == 0), stop=(pair == 1)
+            )
+
+        for h in range(2):
+            add_squares(nc.gpsimd, 0, h)
         yt_grouped = yt_mx[0][:].rearrange("p (j m) -> p j m", m=PACK)
         for b in range(TILES):
             nc.vector.tensor_tensor(
@@ -176,23 +192,9 @@ def tile_nntransformlearner_pa_s_kernel(tc, x_base, y, R, t, out):
                 in1=t32[:].unsqueeze(1).to_broadcast([P, P, PACK]),
                 op=ALU.add,
             )
-
-        yn_acc = [psum.tile([P, PAIR], F32, name="yn_acc", tag="bank") for h in range(2)]
-        for pair in range(2):
-            for h in range(2):
-                cols = slice(h * PAIR, (h + 1) * PAIR)
-                adder = nc.vector if (pair, h) == (1, 1) else nc.gpsimd
-                adder.tensor_tensor(
-                    out=squares[2 * pair][:, cols],
-                    in0=squares[2 * pair][:, cols],
-                    in1=squares[2 * pair + 1][:, cols],
-                    op=ALU.add,
-                )
-                nc.tensor.matmul(
-                    out=yn_acc[h][:], lhsT=ones[:, 0:P], rhs=squares[2 * pair][:, cols], start=(pair == 0), stop=(pair == 1)
-                )
-        quantise(yt_mx, 0)
-        quantise(yt_mx, 1)
+            if b >= 2:
+                add_squares(nc.vector, 1, b - 2)
+        nc.vector.quantize_mx(out=yt_mx[1][:].bitcast(FP8X4), scales=yt_mx[2][:], in_=yt_mx[0][:])
         quantise(x_mx, 1)
         xn_scaled = keep.tile([P, TILES], F32, name="xn_scaled")
         for h in range(2):

@@ -17,6 +17,7 @@ SIZE = 512
 TILES = SIZE // P
 PAIR = 2 * P
 GAMMA = 1.0 / 256.0
+FILL = 2
 LAG = 2
 
 FLOPS = 2 * 2 * SIZE * SIZE * SIZE
@@ -70,6 +71,8 @@ def tile_nntransformlearner_pa_s_kernel(tc, x_base, y, R, t, out):
                     nc.tensor.transpose(
                         flipped[:, u, a * P : (a + 1) * P], row_words[:, u * P : (u + 1) * P], ident[:]
                     )
+            for rep in range(FILL):
+                nc.tensor.transpose(idle[:, 0:P], ident[:], ident[:])
             return flipped
 
         def operand(name):

@@ -50,10 +50,10 @@ def tile_nntransformlearner_pa_s_kernel(tc, x_base, y, R, t, out):
         for h in range(2):
             nc.sync.dma_start(out=x_sb[:, 2 * h : 2 * h + 2, :].rearrange("p a d -> p (a d)"), in_=x_rows[h])
 
+        ones = keep.tile([P, PAIR], F32, name="ones")
+        nc.gpsimd.memset(ones[:], 1.0)
         ident = keep.tile([P, P], F32, name="ident")
         make_identity(nc, ident[:])
-        ones = keep.tile([P, PAIR], F32, name="ones")
-        nc.vector.memset(ones[:], 1.0)
         idle = psum.tile([P, PAIR], F32, name="idle", tag="bank")
         for rep in range(2):
             nc.tensor.matmul(out=idle[:], lhsT=ones[:, 0:P], rhs=ones[:], start=True, stop=True)
@@ -63,7 +63,7 @@ def tile_nntransformlearner_pa_s_kernel(tc, x_base, y, R, t, out):
         t32 = keep.tile([P, PACK], F32, name="t32")
         nc.vector.tensor_copy(out=t32[:], in_=t_sb[:])
 
-        def flip(rows_sb, h):
+        def flip(rows_sb, h, fill=FILL):
             flipped = psum.tile([P, 2, PAIR], F32, name="flipped", tag="bank")
             for a in range(2):
                 row_words = rows_sb[:, 2 * h + a, :].bitcast(F32)
@@ -71,7 +71,7 @@ def tile_nntransformlearner_pa_s_kernel(tc, x_base, y, R, t, out):
                     nc.tensor.transpose(
                         flipped[:, u, a * P : (a + 1) * P], row_words[:, u * P : (u + 1) * P], ident[:]
                     )
-            for rep in range(FILL):
+            for rep in range(fill):
                 nc.tensor.transpose(idle[:, 0:P], ident[:], ident[:])
             return flipped
 
@@ -100,7 +100,7 @@ def tile_nntransformlearner_pa_s_kernel(tc, x_base, y, R, t, out):
         yt_mx = operand("yt")
         y_flipped = [flip(y_sb, h) for h in range(2)]
         r_flipped = [flip(r_sb, h) for h in range(2)]
-        x_flipped = [flip(x_sb, h) for h in range(2)]
+        x_flipped = [flip(x_sb, 0), flip(x_sb, 1, fill=0)]
         regroup(nc.vector.tensor_copy, y_flipped[0], y_mx, 0)
         regroup(nc.scalar.copy, y_flipped[1], y_mx, 1)
         quantise(y_mx, 0)
@@ -167,9 +167,13 @@ def tile_nntransformlearner_pa_s_kernel(tc, x_base, y, R, t, out):
                 for m in (2 * pair, 2 * pair + 1):
                     square(m, slice(h * PAIR, (h + 1) * PAIR))
         xn = keep.tile([P, TILES], F32, name="xn")
-        for a in range(TILES):
+
+        def x_norm(a):
             unused = stage.tile([P, SIZE], BF16, name="unused")
             nc.scalar.activation(out=unused[:], in_=x_sb[:, a, :], func=ACT.Square, accum_out=xn[:, a : a + 1])
+
+        for a in range(TILES - 1):
+            x_norm(a)
 
         yn_acc = [psum.tile([P, PAIR], F32, name="yn_acc", tag="bank") for h in range(2)]
 
@@ -195,18 +199,20 @@ def tile_nntransformlearner_pa_s_kernel(tc, x_base, y, R, t, out):
                 in1=t32[:].unsqueeze(1).to_broadcast([P, P, PACK]),
                 op=ALU.add,
             )
-            if b >= 2:
-                add_squares(nc.vector, 1, b - 2)
+            if b == 2:
+                for h in range(2):
+                    add_squares(nc.vector, 1, h)
         nc.vector.quantize_mx(out=yt_mx[1][:].bitcast(FP8X4), scales=yt_mx[2][:], in_=yt_mx[0][:])
         quantise(x_mx, 1)
+        yn = keep.tile([P, SIZE], F32, name="yn")
+        for h in range(2):
+            nc.scalar.copy(out=yn[:, h * PAIR : (h + 1) * PAIR], in_=yn_acc[h][:])
+        x_norm(TILES - 1)
         xn_scaled = keep.tile([P, TILES], F32, name="xn_scaled")
         for h in range(2):
             nc.gpsimd.tensor_scalar_mul(
                 out=xn_scaled[:, 2 * h : 2 * h + 2], in0=xn[:, 2 * h : 2 * h + 2], scalar1=-GAMMA
             )
-        yn = keep.tile([P, SIZE], F32, name="yn")
-        for h in range(2):
-            nc.vector.tensor_copy(out=yn[:, h * PAIR : (h + 1) * PAIR], in_=yn_acc[h][:])
 
         crosses = []
         for a in range(TILES):

@@ -199,9 +199,8 @@ def tile_nntransformlearner_pa_s_kernel(tc, x_base, y, R, t, out):
                 in1=t32[:].unsqueeze(1).to_broadcast([P, P, PACK]),
                 op=ALU.add,
             )
-            if b == 2:
-                for h in range(2):
-                    add_squares(nc.vector, 1, h)
+            if b >= 2:
+                add_squares(nc.vector, 1, b - 2)
         nc.vector.quantize_mx(out=yt_mx[1][:].bitcast(FP8X4), scales=yt_mx[2][:], in_=yt_mx[0][:])
         quantise(x_mx, 1)
         yn = keep.tile([P, SIZE], F32, name="yn")

@@ -35,18 +35,18 @@ def tile_nntransformlearner_pa_s_kernel(tc, x_base, y, R, t, out):
         r_sb = keep.tile([P, TILES, SIZE], BF16, name="r_sb")
         x_sb = keep.tile([P, TILES, SIZE], BF16, name="x_sb")
         t_sb = keep.tile([P, PACK], BF16, name="t_sb")
-        nc.scalar.dma_start(
-            out=t_sb[:].rearrange("p (u e) -> p u e", u=2),
-            in_=t.rearrange("(u p e) o -> p u (e o)", u=2, e=2),
-        )
-        y_rows = y.rearrange("(h a p) k -> h p a k", h=2, p=P)
+        y_rows = y.rearrange("(h p a) k -> h p (a k)", h=2, a=2)
         r_rows = R.rearrange("(u p e) k -> u p (e k)", u=2, e=2)
         x_rows = x_base.rearrange("(p h a) d -> h p (a d)", h=2, a=2)
         out_rows = out.rearrange("(p a) j -> a p j", a=TILES)
         for h in range(2):
-            nc.sync.dma_start(out=y_sb[:, 2 * h : 2 * h + 2, :], in_=y_rows[h])
+            nc.sync.dma_start(out=y_sb[:, 2 * h : 2 * h + 2, :].rearrange("p a k -> p (a k)"), in_=y_rows[h])
         for h in range(2):
             nc.sync.dma_start(out=r_sb[:, 2 * h : 2 * h + 2, :].rearrange("p e k -> p (e k)"), in_=r_rows[h])
+        nc.sync.dma_start(
+            out=t_sb[:].rearrange("p (u e) -> p u e", u=2),
+            in_=t.rearrange("(u p e) o -> p u (e o)", u=2, e=2),
+        )
         for h in range(2):
             nc.sync.dma_start(out=x_sb[:, 2 * h : 2 * h + 2, :].rearrange("p a d -> p (a d)"), in_=x_rows[h])
 
@@ -60,8 +60,6 @@ def tile_nntransformlearner_pa_s_kernel(tc, x_base, y, R, t, out):
         warm = keep.tile([P, 1], F32, name="warm")
         nc.vector.memset(warm[:], 0.0)
         nc.scalar.activation(out=warm[:], in_=warm[:], func=ACT.Exp)
-        t32 = keep.tile([P, PACK], F32, name="t32")
-        nc.vector.tensor_copy(out=t32[:], in_=t_sb[:])
 
         def flip(rows_sb, h, fill=FILL):
             flipped = psum.tile([P, 2, PAIR], F32, name="flipped", tag="bank")
@@ -81,9 +79,15 @@ def tile_nntransformlearner_pa_s_kernel(tc, x_base, y, R, t, out):
             scales = keep.tile([P, SIZE], U8, align_bytes=64, name=name + "_scales")
             return grouped, codes, scales
 
-        def regroup(copy, flipped, mx, h):
-            words = mx[0][:].bitcast(F32).rearrange("p (c u) -> p c u", u=2)
-            copy(out=words[:, h * PAIR : (h + 1) * PAIR, :], in_=flipped[:].rearrange("p u c -> p c u"))
+        def regroup(copy, flipped, mx, h, pairs=False):
+            words = mx[0][:].bitcast(F32).rearrange("p (c u) -> p c u", u=2)[:, h * PAIR : (h + 1) * PAIR, :]
+            if pairs:
+                copy(
+                    out=words.rearrange("p (c a) u -> p c a u", a=2),
+                    in_=flipped[:].rearrange("p u (a c) -> p c a u", a=2),
+                )
+            else:
+                copy(out=words, in_=flipped[:].rearrange("p u c -> p c u"))
 
         def quantise(mx, h):
             grouped, codes, scales = mx
@@ -101,8 +105,8 @@ def tile_nntransformlearner_pa_s_kernel(tc, x_base, y, R, t, out):
         y_flipped = [flip(y_sb, h) for h in range(2)]
         r_flipped = [flip(r_sb, h) for h in range(2)]
         x_flipped = [flip(x_sb, 0), flip(x_sb, 1, fill=0)]
-        regroup(nc.vector.tensor_copy, y_flipped[0], y_mx, 0)
-        regroup(nc.scalar.copy, y_flipped[1], y_mx, 1)
+        regroup(nc.vector.tensor_copy, y_flipped[0], y_mx, 0, pairs=True)
+        regroup(nc.scalar.copy, y_flipped[1], y_mx, 1, pairs=True)
         quantise(y_mx, 0)
         quantise(y_mx, 1)
         regroup(nc.scalar.copy, r_flipped[0], r_mx, 0)
@@ -159,7 +163,7 @@ def tile_nntransformlearner_pa_s_kernel(tc, x_base, y, R, t, out):
 
         def square(m, cols):
             nc.scalar.activation(
-                out=squares[m][:, cols], in_=by_feature[m][:, cols], func=ACT.Square, bias=t32[:, m : m + 1]
+                out=squares[m][:, cols], in_=by_feature[m][:, cols], func=ACT.Square, bias=t_sb[:, m : m + 1]
             )
 
         for pair in range(2):
@@ -196,7 +200,7 @@ def tile_nntransformlearner_pa_s_kernel(tc, x_base, y, R, t, out):
             nc.vector.tensor_tensor(
                 out=yt_grouped[:, tile_cols(b), :],
                 in0=by_point[b][:].rearrange("p m j -> p j m"),
-                in1=t32[:].unsqueeze(1).to_broadcast([P, P, PACK]),
+                in1=t_sb[:].unsqueeze(1).to_broadcast([P, P, PACK]),
                 op=ALU.add,
             )
             if b >= 2:

@@ -18,7 +18,7 @@ TILES = SIZE // P
 PAIR = 2 * P
 GAMMA = 1.0 / 256.0
 FILL = 2
-LAG = 2
+YN_BANK = (7, 3)
 
 FLOPS = 2 * 2 * SIZE * SIZE * SIZE
 
@@ -28,8 +28,11 @@ def tile_nntransformlearner_pa_s_kernel(tc, x_base, y, R, t, out):
     with ExitStack() as ctx:
         keep = ctx.enter_context(tc.tile_pool(name="keep", bufs=1))
         stage = ctx.enter_context(tc.tile_pool(name="stage", bufs=4))
-        psum = ctx.enter_context(tc.psum_pool(name="psum", bufs=8))
+        psum = ctx.enter_context(tc.psum_pool(name="psum", bufs=1))
         ctx.enter_context(tc.manual_schedule())
+
+        def bank(number, shape, name):
+            return psum.tile(shape, F32, name=name, tag="bank%d" % number)
 
         y_sb = keep.tile([P, TILES, SIZE], BF16, name="y_sb")
         r_sb = keep.tile([P, TILES, SIZE], BF16, name="r_sb")
@@ -38,31 +41,35 @@ def tile_nntransformlearner_pa_s_kernel(tc, x_base, y, R, t, out):
         y_rows = y.rearrange("(h p a) k -> h p (a k)", h=2, a=2)
         r_rows = R.rearrange("(u p e) k -> u p (e k)", u=2, e=2)
         x_rows = x_base.rearrange("(p h a) d -> h p (a d)", h=2, a=2)
-        out_rows = out.rearrange("(p a) j -> a p j", a=TILES)
-        for h in range(2):
-            nc.sync.dma_start(out=y_sb[:, 2 * h : 2 * h + 2, :].rearrange("p a k -> p (a k)"), in_=y_rows[h])
-        for h in range(2):
-            nc.sync.dma_start(out=r_sb[:, 2 * h : 2 * h + 2, :].rearrange("p e k -> p (e k)"), in_=r_rows[h])
+        out_rows = out.rearrange("(p a) j -> p a j", a=TILES)
+
+        def load(rows_sb, rows, h):
+            nc.sync.dma_start(out=rows_sb[:, 2 * h : 2 * h + 2, :].rearrange("p a k -> p (a k)"), in_=rows[h])
+
+        load(y_sb, y_rows, 0)
+        load(r_sb, r_rows, 0)
+        load(r_sb, r_rows, 1)
+        load(y_sb, y_rows, 1)
         nc.sync.dma_start(
             out=t_sb[:].rearrange("p (u e) -> p u e", u=2),
             in_=t.rearrange("(u p e) o -> p u (e o)", u=2, e=2),
         )
-        for h in range(2):
-            nc.sync.dma_start(out=x_sb[:, 2 * h : 2 * h + 2, :].rearrange("p a d -> p (a d)"), in_=x_rows[h])
+        load(x_sb, x_rows, 0)
+        load(x_sb, x_rows, 1)
 
         ones = keep.tile([P, PAIR], F32, name="ones")
         nc.gpsimd.memset(ones[:], 1.0)
         ident = keep.tile([P, P], F32, name="ident")
         make_identity(nc, ident[:])
-        idle = psum.tile([P, PAIR], F32, name="idle", tag="bank")
+        idle = bank(0, [P, PAIR], "idle")
         for rep in range(2):
             nc.tensor.matmul(out=idle[:], lhsT=ones[:, 0:P], rhs=ones[:], start=True, stop=True)
         warm = keep.tile([P, 1], F32, name="warm")
         nc.vector.memset(warm[:], 0.0)
         nc.scalar.activation(out=warm[:], in_=warm[:], func=ACT.Exp)
 
-        def flip(rows_sb, h, fill=FILL):
-            flipped = psum.tile([P, 2, PAIR], F32, name="flipped", tag="bank")
+        def flip(number, rows_sb, h, fill):
+            flipped = bank(number, [P, 2, PAIR], "flipped%d" % number)
             for a in range(2):
                 row_words = rows_sb[:, 2 * h + a, :].bitcast(F32)
                 for u in range(2):
@@ -98,25 +105,6 @@ def tile_nntransformlearner_pa_s_kernel(tc, x_base, y, R, t, out):
                 in_=grouped[:, h * PAIR * PACK : (h + 1) * PAIR * PACK],
             )
 
-        y_mx = operand("y")
-        r_mx = operand("r")
-        x_mx = operand("x")
-        yt_mx = operand("yt")
-        y_flipped = [flip(y_sb, h) for h in range(2)]
-        r_flipped = [flip(r_sb, h) for h in range(2)]
-        x_flipped = [flip(x_sb, 0), flip(x_sb, 1, fill=0)]
-        regroup(nc.vector.tensor_copy, y_flipped[0], y_mx, 0, pairs=True)
-        regroup(nc.scalar.copy, y_flipped[1], y_mx, 1, pairs=True)
-        quantise(y_mx, 0)
-        quantise(y_mx, 1)
-        regroup(nc.scalar.copy, r_flipped[0], r_mx, 0)
-        regroup(nc.scalar.copy, r_flipped[1], r_mx, 1)
-        quantise(r_mx, 0)
-        quantise(r_mx, 1)
-        regroup(nc.scalar.copy, x_flipped[0], x_mx, 0)
-        regroup(nc.vector.tensor_copy, x_flipped[1], x_mx, 1)
-        quantise(x_mx, 0)
-
         def mx_pass(acc, lhs, lhs_cols, rhs, rhs_cols):
             nc.tensor.matmul_mx(
                 out=acc,
@@ -131,112 +119,191 @@ def tile_nntransformlearner_pa_s_kernel(tc, x_base, y, R, t, out):
         def tile_cols(i):
             return slice(i * P, (i + 1) * P)
 
-        every = slice(0, SIZE)
+        def half_cols(h):
+            return slice(h * PAIR, (h + 1) * PAIR)
 
-        by_feature = []
-        by_point = []
+        y_mx = operand("y")
+        r_mx = operand("r")
+        x_mx = operand("x")
+        yt_mx = operand("yt")
+        vector_copy = nc.vector.tensor_copy
+        scalar_copy = nc.scalar.copy
 
-        def feature_pass(m):
-            acc = psum.tile([P, SIZE], F32, name="by_feature", tag="bank")
-            mx_pass(acc[:], r_mx, tile_cols(m), y_mx, every)
-            by_feature.append(acc)
+        y0_flipped = flip(1, y_sb, 0, FILL)
+        r0_flipped = flip(2, r_sb, 0, FILL)
+        r1_flipped = flip(3, r_sb, 1, FILL)
+        y1_flipped = flip(4, y_sb, 1, FILL)
+        x0_flipped = flip(5, x_sb, 0, 0)
+        regroup(scalar_copy, y0_flipped, y_mx, 0, pairs=True)
+        quantise(y_mx, 0)
+        regroup(scalar_copy, r0_flipped, r_mx, 0)
+        quantise(r_mx, 0)
+        regroup(scalar_copy, r1_flipped, r_mx, 1)
+        quantise(r_mx, 1)
+        regroup(scalar_copy, y1_flipped, y_mx, 1, pairs=True)
+        regroup(vector_copy, x0_flipped, x_mx, 0)
+        quantise(y_mx, 1)
 
-        def point_passes(b):
-            acc = psum.tile([P, PACK, P], F32, name="by_point", tag="bank")
+        def feature_passes(number, u, h):
+            acc = bank(number, [P, 2, PAIR], "by_feature%d%d" % (u, h))
+            for e in range(2):
+                mx_pass(acc[:, e, :], r_mx, tile_cols(2 * u + e), y_mx, half_cols(h))
+            return acc
+
+        def point_passes(number, b):
+            acc = bank(number, [P, PACK, P], "by_point%d" % b)
             for m in range(PACK):
                 mx_pass(acc[:, m, :], r_mx, tile_cols(m), y_mx, tile_cols(b))
-            by_point.append(acc)
+            return acc
 
-        feature_pass(0)
-        feature_pass(1)
-        point_passes(0)
-        feature_pass(2)
-        point_passes(1)
-        feature_pass(3)
-        point_passes(2)
-        point_passes(3)
+        by_feature = {}
+        by_point = {}
+        by_feature[0, 0] = feature_passes(6, 0, 0)
+        by_point[0] = point_passes(1, 0)
+        by_feature[1, 0] = feature_passes(7, 1, 0)
+        by_point[1] = point_passes(2, 1)
+        by_feature[0, 1] = feature_passes(3, 0, 1)
+        by_point[2] = point_passes(0, 2)
+        by_feature[1, 1] = feature_passes(6, 1, 1)
+        by_point[3] = point_passes(5, 3)
+        x1_flipped = flip(4, x_sb, 1, 0)
 
-        squares = []
-        for m in range(PACK):
-            sq = keep.tile([P, SIZE], F32, name="sq%d" % m)
-            squares.append(sq)
+        squares = {}
 
-        def square(m, cols):
-            nc.scalar.activation(
-                out=squares[m][:, cols], in_=by_feature[m][:, cols], func=ACT.Square, bias=t_sb[:, m : m + 1]
-            )
+        def square(u, h):
+            sq = keep.tile([P, 2, PAIR], F32, name="sq%d%d" % (u, h))
+            for e in (1, 0):
+                m = 2 * u + e
+                nc.scalar.activation(
+                    out=sq[:, e, :], in_=by_feature[u, h][:, e, :], func=ACT.Square, bias=t_sb[:, m : m + 1]
+                )
+            squares[u, h] = sq
 
-        for pair in range(2):
-            for h in range(2):
-                for m in (2 * pair, 2 * pair + 1):
-                    square(m, slice(h * PAIR, (h + 1) * PAIR))
-        xn = keep.tile([P, TILES], F32, name="xn")
+        def add_squares(adder, u, h):
+            sq = squares[u, h]
+            adder.tensor_tensor(out=sq[:, 0, :], in0=sq[:, 0, :], in1=sq[:, 1, :], op=ALU.add)
 
-        def x_norm(a):
-            unused = stage.tile([P, SIZE], BF16, name="unused")
-            nc.scalar.activation(out=unused[:], in_=x_sb[:, a, :], func=ACT.Square, accum_out=xn[:, a : a + 1])
+        yn_acc = {}
 
-        for a in range(TILES - 1):
-            x_norm(a)
-
-        yn_acc = [psum.tile([P, PAIR], F32, name="yn_acc", tag="bank") for h in range(2)]
-
-        def add_squares(adder, pair, h):
-            cols = slice(h * PAIR, (h + 1) * PAIR)
-            adder.tensor_tensor(
-                out=squares[2 * pair][:, cols],
-                in0=squares[2 * pair][:, cols],
-                in1=squares[2 * pair + 1][:, cols],
-                op=ALU.add,
-            )
+        def over_partitions(u, h):
+            if u == 0:
+                yn_acc[h] = bank(YN_BANK[h], [P, PAIR], "yn_acc%d" % h)
             nc.tensor.matmul(
-                out=yn_acc[h][:], lhsT=ones[:, 0:P], rhs=squares[2 * pair][:, cols], start=(pair == 0), stop=(pair == 1)
+                out=yn_acc[h][:], lhsT=ones[:, 0:P], rhs=squares[u, h][:, 0, :], start=(u == 0), stop=(u == 1)
             )
 
-        for h in range(2):
-            add_squares(nc.gpsimd, 0, h)
+        yn = keep.tile([P, SIZE], F32, name="yn")
+
+        def copy_norms(h):
+            nc.scalar.copy(out=yn[:, half_cols(h)], in_=yn_acc[h][:])
+
         yt_grouped = yt_mx[0][:].rearrange("p (j m) -> p j m", m=PACK)
-        for b in range(TILES):
+
+        def add_t(b):
             nc.vector.tensor_tensor(
                 out=yt_grouped[:, tile_cols(b), :],
                 in0=by_point[b][:].rearrange("p m j -> p j m"),
                 in1=t_sb[:].unsqueeze(1).to_broadcast([P, P, PACK]),
                 op=ALU.add,
             )
-            if b >= 2:
-                add_squares(nc.vector, 1, b - 2)
-        nc.vector.quantize_mx(out=yt_mx[1][:].bitcast(FP8X4), scales=yt_mx[2][:], in_=yt_mx[0][:])
-        quantise(x_mx, 1)
-        yn = keep.tile([P, SIZE], F32, name="yn")
-        for h in range(2):
-            nc.scalar.copy(out=yn[:, h * PAIR : (h + 1) * PAIR], in_=yn_acc[h][:])
-        x_norm(TILES - 1)
+
+        xn = keep.tile([P, TILES], F32, name="xn")
         xn_scaled = keep.tile([P, TILES], F32, name="xn_scaled")
-        for h in range(2):
+
+        def x_norm(a):
+            unused = stage.tile([P, SIZE], BF16, name="unused")
+            nc.scalar.activation(out=unused[:], in_=x_sb[:, a, :], func=ACT.Square, accum_out=xn[:, a : a + 1])
+
+        def scale_norms(h):
             nc.gpsimd.tensor_scalar_mul(
                 out=xn_scaled[:, 2 * h : 2 * h + 2], in0=xn[:, 2 * h : 2 * h + 2], scalar1=-GAMMA
             )
 
-        crosses = []
-        for a in range(TILES):
-            cross = psum.tile([P, SIZE], F32, name="cross", tag="bank")
-            mx_pass(cross[:], x_mx, tile_cols(a), yt_mx, every)
-            crosses.append(cross)
-        pieces = [(a, every) for a in range(TILES - 1)]
-        pieces.extend([(TILES - 1, slice(h * PAIR, (h + 1) * PAIR)) for h in range(2)])
-        results = []
-        for k in range(len(pieces) + LAG):
-            if k < len(pieces):
-                a, cols = pieces[k]
-                part = keep.tile([P, cols.stop - cols.start], F32, name="part%d" % k)
-                nc.vector.scalar_tensor_tensor(
-                    out=part[:], in0=crosses[a][:, cols], scalar=-2.0, in1=yn[:, cols], op0=ALU.mult, op1=ALU.add
+        x_norm(0)
+        square(0, 0)
+        add_squares(nc.gpsimd, 0, 0)
+        add_t(0)
+        square(1, 0)
+        add_squares(nc.gpsimd, 1, 0)
+        add_t(1)
+        quantise(x_mx, 0)
+        square(0, 1)
+        add_t(2)
+        add_squares(nc.vector, 0, 1)
+        square(1, 1)
+        quantise(yt_mx, 0)
+        add_squares(nc.vector, 1, 1)
+        add_t(3)
+        quantise(yt_mx, 1)
+        over_partitions(0, 0)
+        over_partitions(1, 0)
+        regroup(scalar_copy, x1_flipped, x_mx, 1)
+        x_norm(1)
+        scale_norms(0)
+        copy_norms(0)
+        x_norm(2)
+
+        def half_crosses(number, h):
+            acc = bank(number, [P, 2, PAIR], "cross_half%d" % h)
+            for a in range(2):
+                mx_pass(acc[:, a, :], x_mx, tile_cols(a), yt_mx, half_cols(h))
+            return acc
+
+        def full_crosses(number, a):
+            acc = bank(number, [P, 1, SIZE], "cross%d" % a)
+            mx_pass(acc[:, 0, :], x_mx, tile_cols(a), yt_mx, slice(0, SIZE))
+            return acc
+
+        over_partitions(0, 1)
+        crosses0 = half_crosses(1, 0)
+        over_partitions(1, 1)
+        crosses1 = half_crosses(2, 1)
+        copy_norms(1)
+
+        def prepare(acc, cols, name):
+            tiles, width = acc.shape[1], cols.stop - cols.start
+            part = keep.tile([P, tiles, width], F32, name="part_" + name)
+            nc.vector.scalar_tensor_tensor(
+                out=part[:],
+                in0=acc,
+                scalar=-2.0,
+                in1=yn[:, cols].unsqueeze(1).to_broadcast([P, tiles, width]),
+                op0=ALU.mult,
+                op1=ALU.add,
+            )
+            return part
+
+        def kernel_function(part, first, name):
+            g = keep.tile(list(part.shape), F32, name="g_" + name)
+            for i in range(part.shape[1]):
+                a = first + i
+                nc.scalar.activation(
+                    out=g[:, i, :], in_=part[:, i, :], func=ACT.Exp, scale=-GAMMA, bias=xn_scaled[:, a : a + 1]
                 )
-                g = keep.tile([P, cols.stop - cols.start], F32, name="g%d" % k)
-                nc.scalar.activation(out=g[:], in_=part[:], func=ACT.Exp, scale=-GAMMA, bias=xn_scaled[:, a : a + 1])
-                results.append(g)
-            if k >= LAG:
-                a, cols = pieces[k - LAG]
-                g = results[k - LAG]
-                nc.vector.tensor_scalar_min(out=g[:], in0=g[:], scalar1=1.0)
-                nc.sync.dma_start(out=out_rows[a][:, cols], in_=g[:])
+            return g
+
+        def clamp_and_store(g, first, cols):
+            nc.vector.tensor_scalar_min(out=g[:], in0=g[:], scalar1=1.0)
+            nc.sync.dma_start(out=out_rows[:, first : first + g.shape[1], cols], in_=g[:])
+
+        left, right, every = half_cols(0), half_cols(1), slice(0, SIZE)
+        part0 = prepare(crosses0[:], left, "0")
+        quantise(x_mx, 1)
+        crosses2 = full_crosses(6, 2)
+        crosses3 = full_crosses(0, 3)
+        g0 = kernel_function(part0, 0, "0")
+        part1 = prepare(crosses1[:], right, "1")
+        x_norm(3)
+        scale_norms(1)
+        clamp_and_store(g0, 0, left)
+        g1 = kernel_function(part1, 0, "1")
+        part2 = prepare(crosses2[:], every, "2")
+        g2 = kernel_function(part2, 2, "2")
+        part3 = prepare(crosses3[:, :, left], left, "3")
+        clamp_and_store(g1, 0, right)
+        g3 = kernel_function(part3, 3, "3")
+        part4 = prepare(crosses3[:, :, right], right, "4")
+        g4 = kernel_function(part4, 3, "4")
+        clamp_and_store(g2, 2, every)
+        clamp_and_store(g3, 3, left)
+        clamp_and_store(g4, 3, right)

@@ -143,6 +143,7 @@ def tile_nntransformlearner_pa_s_kernel(tc, x_base, y, R, t, out):
         regroup(scalar_copy, y1_flipped, y_mx, 1, pairs=True)
         regroup(vector_copy, x0_flipped, x_mx, 0)
         quantise(y_mx, 1)
+        quantise(x_mx, 0)
 
         def feature_passes(number, u, h):
             acc = bank(number, [P, 2, PAIR], "by_feature%d%d" % (u, h))
@@ -226,14 +227,13 @@ def tile_nntransformlearner_pa_s_kernel(tc, x_base, y, R, t, out):
         square(1, 0)
         add_squares(nc.gpsimd, 1, 0)
         add_t(1)
-        quantise(x_mx, 0)
         square(0, 1)
         add_t(2)
         add_squares(nc.vector, 0, 1)
         square(1, 1)
         quantise(yt_mx, 0)
-        add_squares(nc.vector, 1, 1)
         add_t(3)
+        add_squares(nc.vector, 1, 1)
         quantise(yt_mx, 1)
         over_partitions(0, 0)
         over_partitions(1, 0)

@@ -234,76 +234,65 @@ def tile_nntransformlearner_pa_s_kernel(tc, x_base, y, R, t, out):
         quantise(yt_mx, 0)
         add_t(3)
         add_squares(nc.vector, 1, 1)
-        quantise(yt_mx, 1)
         over_partitions(0, 0)
         over_partitions(1, 0)
         regroup(scalar_copy, x1_flipped, x_mx, 1)
+        quantise(x_mx, 1)
+        quantise(yt_mx, 1)
         x_norm(1)
         scale_norms(0)
         copy_norms(0)
         x_norm(2)
+        x_norm(3)
+        scale_norms(1)
 
-        def half_crosses(number, h):
-            acc = bank(number, [P, 2, PAIR], "cross_half%d" % h)
-            for a in range(2):
-                mx_pass(acc[:, a, :], x_mx, tile_cols(a), yt_mx, half_cols(h))
-            return acc
-
-        def full_crosses(number, a):
-            acc = bank(number, [P, 1, SIZE], "cross%d" % a)
-            mx_pass(acc[:, 0, :], x_mx, tile_cols(a), yt_mx, slice(0, SIZE))
+        def crosses(number, pair, h):
+            acc = bank(number, [P, 2, PAIR], "cross%d%d" % (pair, h))
+            for i in range(2):
+                mx_pass(acc[:, i, :], x_mx, tile_cols(2 * pair + i), yt_mx, half_cols(h))
             return acc
 
         over_partitions(0, 1)
-        crosses0 = half_crosses(1, 0)
+        cross00 = crosses(1, 0, 0)
         over_partitions(1, 1)
-        crosses1 = half_crosses(2, 1)
+        cross10 = crosses(2, 1, 0)
+        cross01 = crosses(6, 0, 1)
+        cross11 = crosses(0, 1, 1)
         copy_norms(1)
 
-        def prepare(acc, cols, name):
-            tiles, width = acc.shape[1], cols.stop - cols.start
-            part = keep.tile([P, tiles, width], F32, name="part_" + name)
+        def kernel_function(acc, first, h):
+            tiles = acc.shape[1]
+            name = "%d%d" % (first, h)
+            part = keep.tile([P, tiles, PAIR], F32, name="part" + name)
             nc.vector.scalar_tensor_tensor(
                 out=part[:],
                 in0=acc,
                 scalar=-2.0,
-                in1=yn[:, cols].unsqueeze(1).to_broadcast([P, tiles, width]),
+                in1=yn[:, half_cols(h)].unsqueeze(1).to_broadcast([P, tiles, PAIR]),
                 op0=ALU.mult,
                 op1=ALU.add,
             )
-            return part
-
-        def kernel_function(part, first, name):
-            g = keep.tile(list(part.shape), F32, name="g_" + name)
-            for i in range(part.shape[1]):
+            g = keep.tile([P, tiles, PAIR], F32, name="g" + name)
+            for i in range(tiles):
                 a = first + i
                 nc.scalar.activation(
                     out=g[:, i, :], in_=part[:, i, :], func=ACT.Exp, scale=-GAMMA, bias=xn_scaled[:, a : a + 1]
                 )
             return g
 
-        def clamp_and_store(g, first, cols):
-            nc.vector.tensor_scalar_min(out=g[:], in0=g[:], scalar1=1.0)
-            nc.sync.dma_start(out=out_rows[:, first : first + g.shape[1], cols], in_=g[:])
+        def clamp_and_store(g, first, h):
+            nc.vector.tensor_scalar_min(out=g, in0=g, scalar1=1.0)
+            nc.sync.dma_start(out=out_rows[:, first : first + g.shape[1], half_cols(h)], in_=g)
 
-        left, right, every = half_cols(0), half_cols(1), slice(0, SIZE)
-        part0 = prepare(crosses0[:], left, "0")
-        quantise(x_mx, 1)
-        crosses2 = full_crosses(6, 2)
-        crosses3 = full_crosses(0, 3)
-        g0 = kernel_function(part0, 0, "0")
-        part1 = prepare(crosses1[:], right, "1")
-        x_norm(3)
-        scale_norms(1)
-        clamp_and_store(g0, 0, left)
-        g1 = kernel_function(part1, 0, "1")
-        part2 = prepare(crosses2[:], every, "2")
-        g2 = kernel_function(part2, 2, "2")
-        part3 = prepare(crosses3[:, :, left], left, "3")
-        clamp_and_store(g1, 0, right)
-        g3 = kernel_function(part3, 3, "3")
-        part4 = prepare(crosses3[:, :, right], right, "4")
-        g4 = kernel_function(part4, 3, "4")
-        clamp_and_store(g2, 2, every)
-        clamp_and_store(g3, 3, left)
-        clamp_and_store(g4, 3, right)
+        g00 = kernel_function(cross00[:], 0, 0)
+        g10 = kernel_function(cross10[:], 2, 0)
+        clamp_and_store(g00[:, 0:1, :], 0, 0)
+        g01 = kernel_function(cross01[:], 0, 1)
+        clamp_and_store(g00[:, 1:2, :], 1, 0)
+        clamp_and_store(g10[:], 2, 0)
+        g31 = kernel_function(cross11[:, 1:2, :], 3, 1)
+        clamp_and_store(g01[:, 0:1, :], 0, 1)
+        g21 = kernel_function(cross11[:, 0:1, :], 2, 1)
+        clamp_and_store(g01[:, 1:2, :], 1, 1)
+        clamp_and_store(g31[:], 3, 1)
+        clamp_and_store(g21[:], 2, 1)

@@ -50,12 +50,12 @@ def tile_nntransformlearner_pa_s_kernel(tc, x_base, y, R, t, out):
         load(r_sb, r_rows, 0)
         load(r_sb, r_rows, 1)
         load(y_sb, y_rows, 1)
+        load(x_sb, x_rows, 0)
+        load(x_sb, x_rows, 1)
         nc.sync.dma_start(
             out=t_sb[:].rearrange("p (u e) -> p u e", u=2),
             in_=t.rearrange("(u p e) o -> p u (e o)", u=2, e=2),
         )
-        load(x_sb, x_rows, 0)
-        load(x_sb, x_rows, 1)
 
         ones = keep.tile([P, PAIR], F32, name="ones")
         nc.gpsimd.memset(ones[:], 1.0)

from contextlib import ExitStack

import concourse.mybir as mybir
from concourse.masks import make_identity

F32 = mybir.dt.float32
BF16 = mybir.dt.bfloat16
U32 = mybir.dt.uint32
U8 = mybir.dt.uint8
FP8X4 = mybir.dt.float8_e4m3fn_x4
ALU = mybir.AluOpType
ACT = mybir.ActivationFunctionType

P = 128
PACK = 4
SIZE = 512
TILES = SIZE // P
PAIR = 2 * P
GAMMA = 1.0 / 256.0
FILL = 2
YN_BANK = (7, 3)

FLOPS = 2 * 2 * SIZE * SIZE * SIZE


def tile_nntransformlearner_pa_s_kernel(tc, x_base, y, R, t, out):
    nc = tc.nc
    with ExitStack() as ctx:
        keep = ctx.enter_context(tc.tile_pool(name="keep", bufs=1))
        stage = ctx.enter_context(tc.tile_pool(name="stage", bufs=4))
        psum = ctx.enter_context(tc.psum_pool(name="psum", bufs=1))
        ctx.enter_context(tc.manual_schedule())

        def bank(number, shape, name):
            return psum.tile(shape, F32, name=name, tag="bank%d" % number)

        y_sb = keep.tile([P, TILES, SIZE], BF16, name="y_sb")
        r_sb = keep.tile([P, TILES, SIZE], BF16, name="r_sb")
        x_sb = keep.tile([P, TILES, SIZE], BF16, name="x_sb")
        t_sb = keep.tile([P, PACK], BF16, name="t_sb")
        y_rows = y.rearrange("(h p a) k -> h p (a k)", h=2, a=2)
        r_rows = R.rearrange("(u p e) k -> u p (e k)", u=2, e=2)
        x_rows = x_base.rearrange("(p h a) d -> h p (a d)", h=2, a=2)
        out_rows = out.rearrange("(p a) j -> p a j", a=TILES)

        def load(rows_sb, rows, h):
            nc.sync.dma_start(out=rows_sb[:, 2 * h : 2 * h + 2, :].rearrange("p a k -> p (a k)"), in_=rows[h])

        load(y_sb, y_rows, 0)
        load(r_sb, r_rows, 0)
        load(r_sb, r_rows, 1)
        load(y_sb, y_rows, 1)
        load(x_sb, x_rows, 0)
        load(x_sb, x_rows, 1)
        nc.sync.dma_start(
            out=t_sb[:].rearrange("p (u e) -> p u e", u=2),
            in_=t.rearrange("(u p e) o -> p u (e o)", u=2, e=2),
        )

        ones = keep.tile([P, PAIR], F32, name="ones")
        nc.gpsimd.memset(ones[:], 1.0)
        ident = keep.tile([P, P], F32, name="ident")
        make_identity(nc, ident[:])
        idle = bank(0, [P, PAIR], "idle")
        for rep in range(2):
            nc.tensor.matmul(out=idle[:], lhsT=ones[:, 0:P], rhs=ones[:], start=True, stop=True)
        warm = keep.tile([P, 1], F32, name="warm")
        nc.vector.memset(warm[:], 0.0)
        nc.scalar.activation(out=warm[:], in_=warm[:], func=ACT.Exp)

        def flip(number, rows_sb, h, fill):
            flipped = bank(number, [P, 2, PAIR], "flipped%d" % number)
            for a in range(2):
                row_words = rows_sb[:, 2 * h + a, :].bitcast(F32)
                for u in range(2):
                    nc.tensor.transpose(
                        flipped[:, u, a * P : (a + 1) * P], row_words[:, u * P : (u + 1) * P], ident[:]
                    )
            for rep in range(fill):
                nc.tensor.transpose(idle[:, 0:P], ident[:], ident[:])
            return flipped

        def operand(name):
            grouped = keep.tile([P, SIZE * PACK], BF16, align_bytes=64, name=name + "_grouped")
            codes = keep.tile([P, SIZE], U32, align_bytes=64, name=name + "_codes")
            scales = keep.tile([P, SIZE], U8, align_bytes=64, name=name + "_scales")
            return grouped, codes, scales

        def regroup(copy, flipped, mx, h, pairs=False):
            words = mx[0][:].bitcast(F32).rearrange("p (c u) -> p c u", u=2)[:, h * PAIR : (h + 1) * PAIR, :]
            if pairs:
                copy(
                    out=words.rearrange("p (c a) u -> p c a u", a=2),
                    in_=flipped[:].rearrange("p u (a c) -> p c a u", a=2),
                )
            else:
                copy(out=words, in_=flipped[:].rearrange("p u c -> p c u"))

        def quantise(mx, h):
            grouped, codes, scales = mx
            cols = slice(h * PAIR, (h + 1) * PAIR)
            nc.vector.quantize_mx(
                out=codes[:, cols].bitcast(FP8X4),
                scales=scales[:, cols],
                in_=grouped[:, h * PAIR * PACK : (h + 1) * PAIR * PACK],
            )

        def mx_pass(acc, lhs, lhs_cols, rhs, rhs_cols):
            nc.tensor.matmul_mx(
                out=acc,
                lhsT=lhs[1][:, lhs_cols].bitcast(FP8X4),
                lhsT_scale=lhs[2][:, lhs_cols],
                rhs=rhs[1][:, rhs_cols].bitcast(FP8X4),
                rhs_scale=rhs[2][:, rhs_cols],
                start=True,
                stop=True,
            )

        def tile_cols(i):
            return slice(i * P, (i + 1) * P)

        def half_cols(h):
            return slice(h * PAIR, (h + 1) * PAIR)

        y_mx = operand("y")
        r_mx = operand("r")
        x_mx = operand("x")
        yt_mx = operand("yt")
        vector_copy = nc.vector.tensor_copy
        scalar_copy = nc.scalar.copy

        y0_flipped = flip(1, y_sb, 0, FILL)
        r0_flipped = flip(2, r_sb, 0, FILL)
        r1_flipped = flip(3, r_sb, 1, FILL)
        y1_flipped = flip(4, y_sb, 1, FILL)
        x0_flipped = flip(5, x_sb, 0, 0)
        regroup(scalar_copy, y0_flipped, y_mx, 0, pairs=True)
        quantise(y_mx, 0)
        regroup(scalar_copy, r0_flipped, r_mx, 0)
        quantise(r_mx, 0)
        regroup(scalar_copy, r1_flipped, r_mx, 1)
        quantise(r_mx, 1)
        regroup(scalar_copy, y1_flipped, y_mx, 1, pairs=True)
        regroup(vector_copy, x0_flipped, x_mx, 0)
        quantise(y_mx, 1)
        quantise(x_mx, 0)

        def feature_passes(number, u, h):
            acc = bank(number, [P, 2, PAIR], "by_feature%d%d" % (u, h))
            for e in range(2):
                mx_pass(acc[:, e, :], r_mx, tile_cols(2 * u + e), y_mx, half_cols(h))
            return acc

        def point_passes(number, b):
            acc = bank(number, [P, PACK, P], "by_point%d" % b)
            for m in range(PACK):
                mx_pass(acc[:, m, :], r_mx, tile_cols(m), y_mx, tile_cols(b))
            return acc

        by_feature = {}
        by_point = {}
        by_feature[0, 0] = feature_passes(6, 0, 0)
        by_point[0] = point_passes(1, 0)
        by_feature[1, 0] = feature_passes(7, 1, 0)
        by_point[1] = point_passes(2, 1)
        by_feature[0, 1] = feature_passes(3, 0, 1)
        by_point[2] = point_passes(0, 2)
        by_feature[1, 1] = feature_passes(6, 1, 1)
        by_point[3] = point_passes(5, 3)
        x1_flipped = flip(4, x_sb, 1, 0)

        squares = {}

        def square(u, h):
            sq = keep.tile([P, 2, PAIR], F32, name="sq%d%d" % (u, h))
            for e in (1, 0):
                m = 2 * u + e
                nc.scalar.activation(
                    out=sq[:, e, :], in_=by_feature[u, h][:, e, :], func=ACT.Square, bias=t_sb[:, m : m + 1]
                )
            squares[u, h] = sq

        def add_squares(adder, u, h):
            sq = squares[u, h]
            adder.tensor_tensor(out=sq[:, 0, :], in0=sq[:, 0, :], in1=sq[:, 1, :], op=ALU.add)

        yn_acc = {}

        def over_partitions(u, h):
            if u == 0:
                yn_acc[h] = bank(YN_BANK[h], [P, PAIR], "yn_acc%d" % h)
            nc.tensor.matmul(
                out=yn_acc[h][:], lhsT=ones[:, 0:P], rhs=squares[u, h][:, 0, :], start=(u == 0), stop=(u == 1)
            )

        yn = keep.tile([P, SIZE], F32, name="yn")

        def copy_norms(h):
            nc.scalar.copy(out=yn[:, half_cols(h)], in_=yn_acc[h][:])

        yt_grouped = yt_mx[0][:].rearrange("p (j m) -> p j m", m=PACK)

        def add_t(b):
            nc.vector.tensor_tensor(
                out=yt_grouped[:, tile_cols(b), :],
                in0=by_point[b][:].rearrange("p m j -> p j m"),
                in1=t_sb[:].unsqueeze(1).to_broadcast([P, P, PACK]),
                op=ALU.add,
            )

        xn = keep.tile([P, TILES], F32, name="xn")
        xn_scaled = keep.tile([P, TILES], F32, name="xn_scaled")

        def x_norm(a):
            unused = stage.tile([P, SIZE], BF16, name="unused")
            nc.scalar.activation(out=unused[:], in_=x_sb[:, a, :], func=ACT.Square, accum_out=xn[:, a : a + 1])

        def scale_norms(h):
            nc.gpsimd.tensor_scalar_mul(
                out=xn_scaled[:, 2 * h : 2 * h + 2], in0=xn[:, 2 * h : 2 * h + 2], scalar1=-GAMMA
            )

        x_norm(0)
        square(0, 0)
        add_squares(nc.gpsimd, 0, 0)
        add_t(0)
        square(1, 0)
        add_squares(nc.gpsimd, 1, 0)
        add_t(1)
        square(0, 1)
        add_t(2)
        add_squares(nc.vector, 0, 1)
        square(1, 1)
        quantise(yt_mx, 0)
        add_t(3)
        add_squares(nc.vector, 1, 1)
        over_partitions(0, 0)
        over_partitions(1, 0)
        regroup(scalar_copy, x1_flipped, x_mx, 1)
        quantise(x_mx, 1)
        quantise(yt_mx, 1)
        x_norm(1)
        scale_norms(0)
        copy_norms(0)
        x_norm(2)
        x_norm(3)
        scale_norms(1)

        def crosses(number, pair, h):
            acc = bank(number, [P, 2, PAIR], "cross%d%d" % (pair, h))
            for i in range(2):
                mx_pass(acc[:, i, :], x_mx, tile_cols(2 * pair + i), yt_mx, half_cols(h))
            return acc

        over_partitions(0, 1)
        cross00 = crosses(1, 0, 0)
        over_partitions(1, 1)
        cross10 = crosses(2, 1, 0)
        cross01 = crosses(6, 0, 1)
        cross11 = crosses(0, 1, 1)
        copy_norms(1)

        def kernel_function(acc, first, h):
            tiles = acc.shape[1]
            name = "%d%d" % (first, h)
            part = keep.tile([P, tiles, PAIR], F32, name="part" + name)
            nc.vector.scalar_tensor_tensor(
                out=part[:],
                in0=acc,
                scalar=-2.0,
                in1=yn[:, half_cols(h)].unsqueeze(1).to_broadcast([P, tiles, PAIR]),
                op0=ALU.mult,
                op1=ALU.add,
            )
            g = keep.tile([P, tiles, PAIR], F32, name="g" + name)
            for i in range(tiles):
                a = first + i
                nc.scalar.activation(
                    out=g[:, i, :], in_=part[:, i, :], func=ACT.Exp, scale=-GAMMA, bias=xn_scaled[:, a : a + 1]
                )
            return g

        def clamp_and_store(g, first, h):
            nc.vector.tensor_scalar_min(out=g, in0=g, scalar1=1.0)
            nc.sync.dma_start(out=out_rows[:, first : first + g.shape[1], half_cols(h)], in_=g)

        g00 = kernel_function(cross00[:], 0, 0)
        g10 = kernel_function(cross10[:], 2, 0)
        clamp_and_store(g00[:, 0:1, :], 0, 0)
        g01 = kernel_function(cross01[:], 0, 1)
        clamp_and_store(g00[:, 1:2, :], 1, 0)
        clamp_and_store(g10[:], 2, 0)
        g31 = kernel_function(cross11[:, 1:2, :], 3, 1)
        clamp_and_store(g01[:, 0:1, :], 0, 1)
        g21 = kernel_function(cross11[:, 0:1, :], 2, 1)
        clamp_and_store(g01[:, 1:2, :], 1, 1)
        clamp_and_store(g31[:], 3, 1)
        clamp_and_store(g21[:], 2, 1)
